import numpy as np
import ml_dtypes


def mxq(x, axis, fmt="e4m3"):
    dtype, down = {"e4m3": (ml_dtypes.float8_e4m3fn, 7), "e5m2": (ml_dtypes.float8_e5m2, 14)}[fmt]
    v = np.moveaxis(np.asarray(x, np.float32).astype(ml_dtypes.bfloat16).astype(np.float64), axis, -1)
    blocks = v.reshape(v.shape[:-1] + (-1, 32))
    amax = np.abs(blocks).max(-1, keepdims=True)
    byte = np.maximum(np.where(amax > 0, np.frexp(amax)[1] - 1 + 127, 0) - down, 1)
    scale = np.exp2(byte - 127.0)
    codes = (blocks / scale).astype(np.float32).astype(dtype).astype(np.float64)
    return np.moveaxis((codes * scale).reshape(v.shape), -1, axis)


WIDE = False


def mx_kscale(k):
    if not WIDE:
        return np.ones(k)
    levels = np.array([10, -10, 5, -5, 0])
    a = np.random.permutation(np.resize(levels, k // 512 * 4)).reshape(k // 512, 4)
    idx = np.arange(k)
    return np.exp2(a[idx // 512, idx % 128 // 32])


BF16 = ml_dtypes.bfloat16


def bf(x):
    return np.asarray(x, np.float32).astype(BF16)


def f64(x):
    return np.asarray(x).astype(np.float64)


E2M1 = np.array([0.0, 0.5, 1.0, 1.5, 2.0, 3.0, 4.0, 6.0, -0.0, -0.5, -1.0, -1.5, -2.0, -3.0, -4.0, -6.0])


def pack_weight(w, fmt):
    k, n = w.shape
    w = f64(bf(w)).reshape(k // 32, 32, n)
    amax = np.abs(w).max(1)
    if fmt == "e4m3":
        byte = np.frexp(amax)[1] - 1 + 127 - 7
    else:
        mant, ex = np.frexp(amax / 6.0)
        byte = np.where(mant > 0.5, ex, ex - 1) + 127
    byte = np.clip(np.where(amax > 0, byte, 1), 1, 254)
    scaled = (w * np.exp2(127.0 - byte)[:, None, :]).reshape(k, n).astype(np.float32)
    by_word = np.ascontiguousarray(scaled.reshape(k // 512, 128, 4, n).transpose(0, 1, 3, 2))
    if fmt == "e4m3":
        words = by_word.astype(ml_dtypes.float8_e4m3fn).view(np.uint8)
    else:
        c = by_word.astype(ml_dtypes.float4_e2m1fn).view(np.uint8) & 0xF
        words = c[..., 0::2] | (c[..., 1::2] << 4)
    return np.ascontiguousarray(words), np.ascontiguousarray(byte.astype(np.uint8).reshape(k // 512, 16, n))


def unpack_weight(words, scales, fmt):
    g, p, n, _ = words.shape
    if fmt == "e4m3":
        vals = np.ascontiguousarray(words).view(ml_dtypes.float8_e4m3fn).astype(np.float64)
    else:
        nib = np.empty((g, p, n, 4), np.uint8)
        nib[..., 0::2] = words & 0xF
        nib[..., 1::2] = words >> 4
        vals = E2M1[nib]
    vals = vals * np.repeat(np.exp2(scales.astype(np.float64) - 127.0), 8, axis=1)[..., None]
    return vals.transpose(0, 1, 3, 2).reshape(g * 512, n)


B, C, O, H, W, KH, KW, PAD = 4, 512, 256, 32, 32, 3, 3, 1
KK = KH * KW
C_CURV = 0.01
EPS = 1e-7


def artanh(z):
    return 0.5 * np.log((1.0 + z) / (1.0 - z))


def log0(y):
    sqc = np.sqrt(C_CURV)
    n = np.maximum(np.sqrt((y * y).sum(-1, keepdims=True)), EPS)
    return artanh(np.clip(sqc * n, 0.0, 1.0 - 1e-6)) * y / (sqc * n)


def exp0(v):
    sqc = np.sqrt(C_CURV)
    n = np.maximum(np.sqrt((v * v).sum(-1, keepdims=True)), EPS)
    return np.tanh(sqc * n) * v / (sqc * n)


def setup_inputs():
    s = mx_kscale(C)
    rho = np.sqrt(np.mean(s * s))
    raw = np.random.uniform(0.0, 1.0, (B, C, H, W)) * s[None, :, None, None]
    r = np.random.uniform(0.2, 0.85, (B, 1, H, W))
    x = raw / np.sqrt((raw * raw).sum(1, keepdims=True)) * r / np.sqrt(C_CURV)
    stack = np.random.standard_normal((KH * KW, O, C)) * 2.1 / np.sqrt(KH * KW * O) * rho / s
    cat = np.swapaxes(stack, 1, 2).reshape(-1, O)
    words, scales = pack_weight(cat, "e4m3")
    return {"x": bf(x),
            "Wk_words": words,
            "Wk_scales": scales,
            "bias": bf(np.random.standard_normal(O) * 5.0 / np.sqrt(O))}


def reference(x, Wk_words, Wk_scales, bias):
    Hout, Wout = H + 2 * PAD - KH + 1, W + 2 * PAD - KW + 1
    u = log0(np.moveaxis(f64(x), 1, -1)).reshape(B * H * W, C)
    w = unpack_weight(Wk_words, Wk_scales, "e4m3").reshape(KK, C, O).transpose(1, 0, 2).reshape(C, KH * KW * O)
    y = mxq(u, 1, "e4m3") @ w
    yp = np.pad(y.reshape(B, H, W, KH * KW, O), ((0, 0), (PAD, PAD), (PAD, PAD), (0, 0), (0, 0)))
    v = sum(yp[:, i:i + Hout, j:j + Wout, KW * i + j, :] for i in range(KH) for j in range(KW))
    v = np.maximum(v + f64(bias), 0.0)
    out = exp0(v)
    return np.transpose(out, (0, 3, 1, 2))

@@ -1,0 +1,519 @@
+from contextlib import ExitStack
+
+from concourse import mybir
+from concourse.masks import make_identity
+
+F32 = mybir.dt.float32
+BF16 = mybir.dt.bfloat16
+I32 = mybir.dt.int32
+U32 = mybir.dt.uint32
+U8 = mybir.dt.uint8
+FP8X4 = mybir.dt.float8_e4m3fn_x4
+ALU = mybir.AluOpType
+ACT = mybir.ActivationFunctionType
+AXIS = mybir.AxisListType
+
+B, C, O, H, W = 4, 512, 256, 32, 32
+TAPS = 3
+P = 128
+PACK = 4
+ROWS = 4
+CHUNKS = H // ROWS
+PIX = ROWS * W
+ROW_COLS = W * B
+CHUNK_COLS = ROWS * ROW_COLS
+O_HALVES = O // P
+CURV = 0.01
+MIN_SQ = 1e-16
+MAX_Z = 1.0 - 1e-6
+
+HEAD_NORMS = 4
+DVE_SHIFTS = 1
+FLIP_LAG = 2
+
+FLOPS = 2 * B * H * W * C * O * TAPS * TAPS
+
+
+def tile_pvconv2d_t_e_kernel(tc, x, Wk_words, Wk_scales, bias, out):
+    nc = tc.nc
+    with ExitStack() as stack:
+        const = stack.enter_context(tc.tile_pool(name="const", bufs=1))
+        small = stack.enter_context(tc.tile_pool(name="small", bufs=3))
+        work = stack.enter_context(tc.tile_pool(name="work", bufs=2))
+        held = stack.enter_context(tc.tile_pool(name="held", bufs=4))
+        stores = stack.enter_context(tc.tile_pool(name="stores", bufs=8))
+        psum = stack.enter_context(tc.psum_pool(name="psum", bufs=1))
+        stack.enter_context(tc.manual_schedule())
+
+        turns = {}
+
+        def bank_tile(banks, shape, name):
+            turn = turns.get(banks, 0)
+            turns[banks] = turn + 1
+            return psum.tile(shape, F32, name=name, tag="bank%d" % banks[turn % len(banks)])
+
+        ACC_BANKS = (0, 1, 2)
+        SPREAD_BANKS = (3, 4)
+        AUX_BANKS = (5, 6, 7)
+        END_BANKS = (3, 4, 5, 6, 7)
+        FIRST_BANKS = (5, 6, 7, 0)
+
+        w_planes = const.tile([P, TAPS, TAPS, O], U8, align_bytes=64)
+        nc.vector.memset(w_planes[:].bitcast(I32), 0)
+        w_words = const.tile([P, TAPS, TAPS, O * PACK], U8, align_bytes=64)
+        bias_rows = const.tile([P, O], BF16)
+        ident = const.tile([P, P], F32)
+        make_identity(nc, ident[:])
+        minus_half = const.tile([P, 4 * B], F32)
+        nc.vector.memset(minus_half[:], -0.5)
+        ones = const.tile([P, 1], F32)
+        nc.vector.memset(ones[:], 1.0)
+        ln_ones = const.tile([P, 1], F32)
+        nc.scalar.activation(out=ln_ones[:], in_=ones[:], func=ACT.Ln)
+        norm_sq = const.tile([P, CHUNKS, B], F32)
+        log_factor = const.tile([P, CHUNKS, B], F32)
+
+        words = []
+        planes = []
+        for v in range(TAPS):
+            words.append(const.tile([P, H * ROW_COLS], U32, name="words%d" % v, align_bytes=64))
+            planes.append(const.tile([P, H * ROW_COLS], U8, name="planes%d" % v, align_bytes=64))
+
+        def chunk_cols(k):
+            return slice(k * CHUNK_COLS, (k + 1) * CHUNK_COLS)
+
+        def word_rows(v, k):
+            return words[v][:, chunk_cols(k)].bitcast(I32).rearrange("p (r n) -> p r n", r=ROWS)
+
+        def plane_rows(v, k):
+            return planes[v][:, chunk_cols(k)].bitcast(I32).rearrange("p (r n) -> p r n", r=ROWS)
+
+        nc.vector.memset(words[0][:].bitcast(I32).rearrange("p (h n) -> p h n", h=H)[:, :, 0:B], 0)
+        nc.vector.memset(planes[0][:].bitcast(I32).rearrange("p (h n) -> p h n", h=H)[:, :, 0:1], 0)
+        nc.vector.memset(words[2][:].bitcast(I32).rearrange("p (h n) -> p h n", h=H)[:, :, ROW_COLS - B : ROW_COLS], 0)
+        nc.vector.memset(planes[2][:].bitcast(I32).rearrange("p (h n) -> p h n", h=H)[:, :, W - 1 : W], 0)
+
+        x_chunks = {}
+
+        def load_x(k, count):
+            x_tile = const.tile([P, B, PACK, count * PIX], BF16, name="x_tile%d" % k)
+            for b in range(B):
+                nc.sync.dma_start(
+                    out=x_tile[:, b, :, :],
+                    in_=x[b].rearrange("(p j) h w -> p j (h w)", j=PACK)[:, :, k * PIX : (k + count) * PIX],
+                )
+            for n in range(count):
+                x_chunks[k + n] = x_tile[:, :, :, n * PIX : (n + 1) * PIX]
+
+        load_x(0, 1)
+        load_x(1, 2)
+        for j in (1, 0, 2):
+            for quad in range(4):
+                nc.sync.dma_start(
+                    out=w_planes[32 * quad : 32 * quad + 4, j, :, :].bitcast(I32),
+                    in_=Wk_scales[j :: TAPS, 4 * quad : 4 * quad + 4, :].rearrange("i r n -> r i n").bitcast(I32),
+                )
+        for j in (1, 0, 2):
+            nc.sync.dma_start(
+                out=w_words[:, j, :, :].bitcast(I32),
+                in_=Wk_words[j :: TAPS].rearrange("i p n t -> p i (n t)").bitcast(I32),
+            )
+        load_x(3, CHUNKS - 3)
+        nc.sync.dma_start(out=bias_rows[:], in_=bias.partition_broadcast(P))
+
+        def inverse_root(square_sum, width, name):
+            y_sq = small.tile([P, width], F32, name=name + "_sq")
+            nc.gpsimd.tensor_scalar(
+                out=y_sq[:], in0=square_sum, scalar1=CURV, scalar2=MIN_SQ, op0=ALU.mult, op1=ALU.max
+            )
+            y_inv = small.tile([P, width], F32, name=name + "_inv")
+            nc.gpsimd.tensor_tensor(out=y_inv[:], in0=y_sq[:], in1=minus_half[:, 0:width], op=ALU.pow)
+            y = small.tile([P, width], F32, name=name)
+            nc.gpsimd.tensor_tensor(out=y[:], in0=y_sq[:], in1=y_inv[:], op=ALU.mult)
+            return y, y_inv
+
+        grams = {}
+
+        def gram(k):
+            grams[k] = bank_tile(AUX_BANKS, [P, B, PIX], "gram%d" % k)
+            for b in range(B):
+                for j in range(PACK):
+                    nc.tensor.matmul(
+                        out=grams[k][:, b, :],
+                        lhsT=x_chunks[k][:, b, j, :],
+                        rhs=x_chunks[k][:, b, j, :],
+                        start=(j == 0),
+                        stop=(j == PACK - 1),
+                    )
+
+        def norm_by_image(k):
+            for b in range(B):
+                gram_b = bank_tile(FIRST_BANKS, [P, PIX], "gram%d_%d" % (k, b))
+                for j in range(PACK):
+                    nc.tensor.matmul(
+                        out=gram_b[:],
+                        lhsT=x_chunks[k][:, b, j, :],
+                        rhs=x_chunks[k][:, b, j, :],
+                        start=(j == 0),
+                        stop=(j == PACK - 1),
+                    )
+                masked = work.tile([P, PIX], F32, name="masked")
+                nc.vector.scalar_tensor_tensor(
+                    out=masked[:], in0=gram_b[:], scalar=1.0, in1=ident[:], op0=ALU.mult, op1=ALU.mult,
+                    accum_out=norm_sq[:, k, b : b + 1],
+                )
+
+        diagonals = {}
+        gram_copies = {}
+
+        def mask(k):
+            diagonals[k] = work.tile([P, B, PIX], F32, name="diagonal%d" % k, tag="diagonal")
+            nc.vector.tensor_tensor(
+                out=diagonals[k][:], in0=grams[k][:], in1=ident[:].unsqueeze(1).to_broadcast([P, B, PIX]), op=ALU.mult
+            )
+
+        def gram_out(k):
+            gram_copies[k] = work.tile([P, B, PIX], F32, name="gram_copy%d" % k, tag="gram_copy")
+            nc.scalar.copy(out=gram_copies[k][:], in_=grams[k][:])
+
+        def mask_pool(k):
+            diagonals[k] = work.tile([P, B, PIX], F32, name="diagonal%d" % k, tag="diagonal")
+            nc.gpsimd.tensor_tensor(
+                out=diagonals[k][:], in0=gram_copies[k][:], in1=ident[:].unsqueeze(1).to_broadcast([P, B, PIX]), op=ALU.mult
+            )
+
+        def reduce_vector(k):
+            nc.vector.tensor_reduce(out=norm_sq[:, k, :], in_=diagonals[k][:], axis=AXIS.X, op=ALU.add)
+
+        def reduce_scalar(k):
+            dropped = work.tile([P, B, PIX], F32, name="dropped")
+            for b in range(B):
+                nc.scalar.activation(
+                    out=dropped[:, b, :], in_=diagonals[k][:, b, :], func=ACT.Copy, accum_out=norm_sq[:, k, b : b + 1]
+                )
+
+        def log_chain(k0, k1):
+            width = (k1 - k0) * B
+            z, z_inv = inverse_root(norm_sq[:, k0:k1, :].rearrange("p k b -> p (k b)"), width, "z")
+            z_clip = small.tile([P, width], F32, name="z_clip")
+            nc.gpsimd.tensor_scalar(
+                out=z_clip[:], in0=z[:], scalar1=MAX_Z, scalar2=0.0, op0=ALU.min, op1=ALU.max
+            )
+            ln_plus = small.tile([P, width], F32, name="ln_plus")
+            nc.scalar.activation(out=ln_plus[:], in_=z_clip[:], func=ACT.Ln, bias=1.0, scale=1.0)
+            ln_minus = small.tile([P, width], F32, name="ln_minus")
+            nc.scalar.activation(out=ln_minus[:], in_=z_clip[:], func=ACT.Ln, bias=1.0, scale=-1.0)
+            half_z_inv = small.tile([P, width], F32, name="half_z_inv")
+            nc.gpsimd.tensor_scalar(
+                out=half_z_inv[:], in0=z_inv[:], scalar1=0.5, scalar2=0.0, op0=ALU.mult, op1=ALU.add
+            )
+            ln_diff = small.tile([P, width], F32, name="ln_diff")
+            nc.gpsimd.tensor_tensor(out=ln_diff[:], in0=ln_plus[:], in1=ln_minus[:], op=ALU.subtract)
+            nc.gpsimd.tensor_tensor(
+                out=log_factor[:, k0:k1, :].rearrange("p k b -> p (k b)"), in0=ln_diff[:], in1=half_z_inv[:], op=ALU.mult
+            )
+
+        spread_factor = {}
+
+        def spread(k):
+            spread_factor[k] = bank_tile(SPREAD_BANKS, [P, B, PIX], "spread%d" % k)
+            for b in range(B):
+                nc.tensor.transpose(
+                    out=spread_factor[k][:, b, :],
+                    in_=log_factor[:, k, b : b + 1].to_broadcast([P, P]),
+                    identity=ident[:],
+                )
+
+        grouped = {}
+        RUN = 4
+
+        products = {}
+
+        def multiply(k):
+            products[k] = work.tile([P, B, PACK, PIX], BF16, name="product%d" % k, tag="product")
+            nc.vector.tensor_tensor(
+                out=products[k][:],
+                in0=x_chunks[k],
+                in1=spread_factor[k][:].unsqueeze(2).to_broadcast([P, B, PACK, PIX]),
+                op=ALU.mult,
+            )
+
+        def order(k):
+            grouped[k] = work.tile([P, PIX, B, PACK], BF16, name="grouped%d" % k, tag="grouped", align_bytes=64)
+            nc.vector.tensor_copy(
+                out=grouped[k][:].rearrange("p (c i) b j -> p c (b j) i", i=RUN),
+                in_=products[k][:].rearrange("p b j (c i) -> p c (b j) i", i=RUN),
+            )
+
+        def quant(k):
+            nc.vector.quantize_mx(
+                out=words[1][:, chunk_cols(k)].bitcast(FP8X4),
+                scales=planes[1][:, chunk_cols(k)],
+                in_=grouped[k][:].rearrange("p q b j -> p (q b j)"),
+            )
+
+        def shift(k):
+            moves = (
+                (word_rows(0, k)[:, :, B:ROW_COLS], word_rows(1, k)[:, :, 0 : ROW_COLS - B]),
+                (word_rows(2, k)[:, :, 0 : ROW_COLS - B], word_rows(1, k)[:, :, B:ROW_COLS]),
+                (plane_rows(0, k)[:, :, 1:W], plane_rows(1, k)[:, :, 0 : W - 1]),
+                (plane_rows(2, k)[:, :, 0 : W - 1], plane_rows(1, k)[:, :, 1:W]),
+            )
+            for dst, src in moves:
+                if k < DVE_SHIFTS:
+                    nc.vector.tensor_copy(out=dst, in_=src)
+                else:
+                    nc.sync.dma_start(out=dst, in_=src)
+
+        biased = {}
+        out_norm_sq = {}
+        accs = {}
+
+        def conv(k, r0, r1):
+            acc = bank_tile(ACC_BANKS, [P, 2, O], "acc%d_%d" % (k, r0))
+            accs[(k, r0)] = acc
+            h = k * ROWS + r0
+            passes = []
+            for j in (1, 0, 2):
+                passes.append((h, j, 0, 2))
+            for j in (1, 0, 2):
+                if h - 1 >= 0:
+                    passes.append((h - 1, j, 0, 1))
+            for j in (1, 0):
+                passes.append((h + 1, j, 1, 3))
+            for j in (1, 0, 2):
+                if h + 2 < H:
+                    passes.append((h + 2, j, 2, 3))
+            passes.append((h + 1, 2, 1, 3))
+            for n, (s, j, i0, i1) in enumerate(passes):
+                cols = slice(s * ROW_COLS, (s + 1) * ROW_COLS)
+                if i1 - i0 == 2:
+                    target = acc[:].rearrange("p r o -> p (r o)")
+                elif s < h:
+                    target = acc[:, 1, :]
+                else:
+                    target = acc[:, 0, :]
+                nc.tensor.matmul_mx(
+                    out=target,
+                    lhsT=words[j][:, cols].bitcast(FP8X4),
+                    lhsT_scale=planes[j][:, cols],
+                    rhs=w_words[:, j, i0:i1, :].rearrange("p i n -> p (i n)").bitcast(FP8X4),
+                    rhs_scale=w_planes[:, j, i0:i1, :].rearrange("p i n -> p (i n)"),
+                    start=(n == 0),
+                    stop=(n == len(passes) - 1),
+                )
+
+        def bias_add(k, r0, r1):
+            if r0 == 0:
+                biased[k] = held.tile([P, ROWS, O], F32, name="biased%d" % k, tag="biased")
+                out_norm_sq[k] = held.tile([P, ROWS], F32, name="out_norm_sq%d" % k, tag="out_norm_sq")
+            nc.vector.tensor_tensor(
+                out=biased[k][:, r0:r1, :],
+                in0=accs[(k, r0)][:],
+                in1=bias_rows[:].unsqueeze(1).to_broadcast([P, r1 - r0, O]),
+                op=ALU.add,
+            )
+
+        def relu_sq(k, r0, r1, on_vector=False):
+            squares = work.tile([P, 2, O], F32, name="squares")
+            if on_vector:
+                for r in range(r0, r1):
+                    nc.vector.scalar_tensor_tensor(
+                        out=squares[:, r - r0, :],
+                        in0=biased[k][:, r, :],
+                        scalar=0.0,
+                        in1=biased[k][:, r, :],
+                        op0=ALU.max,
+                        op1=ALU.mult,
+                        accum_out=out_norm_sq[k][:, r : r + 1],
+                    )
+                return
+            relu = work.tile([P, 2, O], F32, name="relu")
+            nc.scalar.activation(out=relu[:, 0 : r1 - r0, :], in_=biased[k][:, r0:r1, :], func=ACT.Relu)
+            for r in range(r0, r1):
+                nc.scalar.activation(
+                    out=squares[:, r - r0, :],
+                    in_=relu[:, r - r0, :],
+                    func=ACT.Square,
+                    accum_out=out_norm_sq[k][:, r : r + 1],
+                )
+
+        exp_factor = {}
+        exp_parts = {}
+
+        def exp_chain_a(k, r0, r1, short=False):
+            width = r1 - r0
+            y_sq = small.tile([P, width], F32, name="y_sq")
+            nc.gpsimd.tensor_scalar(
+                out=y_sq[:], in0=out_norm_sq[k][:, r0:r1], scalar1=CURV, scalar2=MIN_SQ, op0=ALU.mult, op1=ALU.max
+            )
+            y_inv = held.tile([P, width], F32, name="y_inv%d_%d" % (k, r0), tag="y_inv")
+            nc.gpsimd.tensor_tensor(out=y_inv[:], in0=y_sq[:], in1=minus_half[:, 0:width], op=ALU.pow)
+            if not short:
+                y = small.tile([P, width], F32, name="y")
+                nc.gpsimd.tensor_tensor(out=y[:], in0=y_sq[:], in1=y_inv[:], op=ALU.mult)
+                y_sq = y
+            exp_parts[(k, r0)] = (y_sq, y_inv)
+
+        def exp_chain_b(k, r0, r1, short=False):
+            y_sq, y_inv = exp_parts[(k, r0)]
+            tanh_y = held.tile([P, r1 - r0], F32, name="tanh_y%d_%d" % (k, r0), tag="tanh_y")
+            if short:
+                for r in range(r1 - r0):
+                    nc.scalar.activation(
+                        out=tanh_y[:, r : r + 1], in_=y_sq[:, r : r + 1], func=ACT.Tanh, scale=y_inv[:, r : r + 1]
+                    )
+            else:
+                nc.scalar.activation(out=tanh_y[:], in_=y_sq[:], func=ACT.Tanh)
+            exp_parts[(k, r0)] = (tanh_y, y_inv)
+            if not short:
+                exp_factor[(k, r0)] = held.tile([P, r1 - r0], F32, name="exp_factor%d_%d" % (k, r0), tag="exp_factor")
+                nc.gpsimd.tensor_tensor(out=exp_factor[(k, r0)][:], in0=tanh_y[:], in1=y_inv[:], op=ALU.mult)
+
+        scaled = {}
+
+        def rescale(k, r0, r1, on_vector=False):
+            if r0 == 0:
+                scaled[k] = work.tile([P, ROWS, O], F32, name="scaled%d" % k, tag="scaled")
+            for r in range(r0, r1):
+                if on_vector:
+                    tanh_y, y_inv = exp_parts[(k, r0)]
+                    nc.vector.tensor_scalar(
+                        out=scaled[k][:, r, :], in0=biased[k][:, r, :], scalar1=tanh_y[:, r - r0 : r - r0 + 1],
+                        scalar2=y_inv[:, r - r0 : r - r0 + 1], op0=ALU.mult, op1=ALU.mult,
+                    )
+                else:
+                    nc.scalar.activation(
+                        out=scaled[k][:, r, :], in_=biased[k][:, r, :], func=ACT.Copy,
+                        scale=exp_factor[(k, r0)][:, r - r0 : r - r0 + 1],
+                    )
+
+        flipped = {}
+
+        def flip(k, r0, r1):
+            for half_o in range(O_HALVES):
+                o_cols = slice(half_o * P, (half_o + 1) * P)
+                flipped[(k, r0, half_o)] = bank_tile(
+                    AUX_BANKS if k + 4 < CHUNKS else END_BANKS, [P, r1 - r0, ROW_COLS], "flipped%d_%d_%d" % (k, r0, half_o)
+                )
+                for r in range(r0, r1):
+                    nc.tensor.transpose(
+                        out=flipped[(k, r0, half_o)][:, r - r0, :], in_=scaled[k][:, r + 1 - 2 * (r % 2), o_cols], identity=ident[:]
+                    )
+
+        def evac(k, r0, r1, share=False, halves=(0, 1)):
+            for half_o in halves:
+                o_cols = slice(half_o * P, (half_o + 1) * P)
+                result = stores.tile([P, B, r1 - r0, W], F32, name="result")
+                turned = flipped[(k, r0, half_o)][:].rearrange("p r (w b) -> p b r w", b=B)
+                if share and half_o == 1:
+                    nc.vector.tensor_scalar(out=result[:], in0=turned, scalar1=0.0, scalar2=0.0, op0=ALU.max, op1=ALU.add)
+                    nc.sync.dma_start(
+                        out=out[:, o_cols, k * ROWS + r0 : k * ROWS + r1, :].rearrange("b p h w -> p b (h w)"),
+                        in_=result[:].rearrange("p b r w -> p b (r w)"),
+                    )
+                else:
+                    nc.scalar.activation(out=result[:], in_=turned, func=ACT.Relu)
+                    nc.sync.dma_start(
+                        out=out[:, o_cols, k * ROWS + r0 : k * ROWS + r1, :].rearrange("b p h w -> p b (h w)"),
+                        in_=result[:].rearrange("p b r w -> p b (r w)"),
+                    )
+
+        last = CHUNKS - 1
+
+        norm_by_image(0)
+        log_chain(0, 1)
+        gram(1)
+        mask(1)
+        reduce_scalar(1)
+        gram(2)
+        spread(0)
+        multiply(0)
+        log_chain(1, 2)
+        order(0)
+        quant(0)
+        shift(0)
+        mask(2)
+        reduce_scalar(2)
+        spread(1)
+        multiply(1)
+        log_chain(2, 3)
+        order(1)
+        flips = []
+        for k in range(CHUNKS):
+            free = k + 2 >= CHUNKS
+            conv(k, 0, 2)
+            if k == 0:
+                gram(3)
+                quant(1)
+                shift(1)
+                mask(3)
+                reduce_scalar(3)
+                gram(4)
+                bias_add(k, 0, 2)
+                mask(4)
+                reduce_scalar(4)
+                log_chain(3, 5)
+                relu_sq(k, 0, 2, True)
+                gram(5)
+                spread(2)
+                multiply(2)
+                mask(5)
+                reduce_scalar(5)
+                gram(6)
+                order(2)
+                mask(6)
+                reduce_scalar(6)
+                gram(7)
+                quant(2)
+                shift(2)
+                mask(7)
+                reduce_scalar(7)
+                log_chain(5, 8)
+                tanh_ones = const.tile([P, 1], F32)
+                nc.scalar.activation(out=tanh_ones[:], in_=ones[:], func=ACT.Tanh)
+            else:
+                bias_add(k - 1, 2, 4)
+                if k + 2 < CHUNKS:
+                    multiply(k + 2)
+                for f in flips:
+                    evac(f, 0, ROWS)
+                flips.clear()
+                relu_sq(k - 1, 2, 4, True)
+                exp_chain_a(k - 1, 0, ROWS, free)
+                if k + 2 < CHUNKS:
+                    order(k + 2)
+                bias_add(k, 0, 2)
+                if k + 2 < CHUNKS:
+                    quant(k + 2)
+                    shift(k + 2)
+                relu_sq(k, 0, 2, True)
+                exp_chain_b(k - 1, 0, ROWS, free)
+                rescale(k - 1, 0, ROWS, free)
+            if k == last:
+                exp_chain_a(last, 0, 2, True)
+                exp_chain_b(last, 0, 2, True)
+            conv(k, 2, 4)
+            if k + 3 < CHUNKS:
+                spread(k + 3)
+                ready = [k - 2] if k >= 2 else []
+            elif k + 3 == CHUNKS:
+                ready = [k - 2]
+            elif k + 2 == CHUNKS:
+                ready = [k - 2, k - 1]
+            else:
+                ready = [k - 1]
+            for f in ready:
+                flip(f, 0, ROWS)
+                flips.append(f)
+        bias_add(last, 2, 4)
+        relu_sq(last, 2, 4, True)
+        exp_chain_a(last, 2, 4, True)
+        rescale(last, 0, 2, True)
+        evac(last - 1, 0, ROWS)
+        exp_chain_b(last, 2, 4, True)
+        flip(last, 0, 2)
+        rescale(last, 2, 4, True)
+        evac(last, 0, 2, True)
+        flip(last, 2, 4)
+        evac(last, 2, 4, True)

@@ -213,36 +213,27 @@ def tile_pvconv2d_t_e_kernel(tc, x, Wk_words, Wk_scales, bias, out):
                 out=log_factor[:, k0:k1, :].rearrange("p k b -> p (k b)"), in0=ln_diff[:], in1=half_z_inv[:], op=ALU.mult
             )
 
+        RUN = 4
         spread_factor = {}
 
         def spread(k):
-            spread_factor[k] = bank_tile(SPREAD_BANKS, [P, B, PIX], "spread%d" % k)
+            spread_factor[k] = bank_tile(SPREAD_BANKS, [P, PIX // RUN, B, RUN], "spread%d" % k)
             for b in range(B):
                 nc.tensor.transpose(
-                    out=spread_factor[k][:, b, :],
+                    out=spread_factor[k][:, :, b, :],
                     in_=log_factor[:, k, b : b + 1].to_broadcast([P, P]),
                     identity=ident[:],
                 )
 
         grouped = {}
-        RUN = 4
-
-        products = {}
 
         def multiply(k):
-            products[k] = work.tile([P, B, PACK, PIX], BF16, name="product%d" % k, tag="product")
-            nc.vector.tensor_tensor(
-                out=products[k][:],
-                in0=x_chunks[k],
-                in1=spread_factor[k][:].unsqueeze(2).to_broadcast([P, B, PACK, PIX]),
-                op=ALU.mult,
-            )
-
-        def order(k):
             grouped[k] = work.tile([P, PIX, B, PACK], BF16, name="grouped%d" % k, tag="grouped", align_bytes=64)
-            nc.vector.tensor_copy(
-                out=grouped[k][:].rearrange("p (c i) b j -> p c (b j) i", i=RUN),
-                in_=products[k][:].rearrange("p b j (c i) -> p c (b j) i", i=RUN),
+            nc.vector.tensor_tensor(
+                out=grouped[k][:].rearrange("p (c i) b j -> p c b j i", i=RUN),
+                in0=x_chunks[k].rearrange("p b j (c i) -> p c b j i", i=RUN),
+                in1=spread_factor[k][:].unsqueeze(3).to_broadcast([P, PIX // RUN, B, PACK, RUN]),
+                op=ALU.mult,
             )
 
         def quant(k):
@@ -430,7 +421,6 @@ def tile_pvconv2d_t_e_kernel(tc, x, Wk_words, Wk_scales, bias, out):
         spread(0)
         multiply(0)
         log_chain(1, 2)
-        order(0)
         quant(0)
         shift(0)
         mask(2)
@@ -438,7 +428,6 @@ def tile_pvconv2d_t_e_kernel(tc, x, Wk_words, Wk_scales, bias, out):
         spread(1)
         multiply(1)
         log_chain(2, 3)
-        order(1)
         flips = []
         for k in range(CHUNKS):
             free = k + 2 >= CHUNKS
@@ -461,7 +450,6 @@ def tile_pvconv2d_t_e_kernel(tc, x, Wk_words, Wk_scales, bias, out):
                 mask(5)
                 reduce_scalar(5)
                 gram(6)
-                order(2)
                 mask(6)
                 reduce_scalar(6)
                 gram(7)
@@ -482,11 +470,9 @@ def tile_pvconv2d_t_e_kernel(tc, x, Wk_words, Wk_scales, bias, out):
                 relu_sq(k - 1, 2, 4, True)
                 exp_chain_a(k - 1, 0, ROWS, free)
                 if k + 2 < CHUNKS:
-                    order(k + 2)
-                bias_add(k, 0, 2)
-                if k + 2 < CHUNKS:
                     quant(k + 2)
                     shift(k + 2)
+                bias_add(k, 0, 2)
                 relu_sq(k, 0, 2, True)
                 exp_chain_b(k - 1, 0, ROWS, free)
                 rescale(k - 1, 0, ROWS, free)

@@ -56,7 +56,8 @@ def tile_pvconv2d_t_e_kernel(tc, x, Wk_words, Wk_scales, bias, out):
         SPREAD_BANKS = (3, 4)
         AUX_BANKS = (5, 6, 7)
         END_BANKS = (3, 4, 5, 6, 7)
-        FIRST_BANKS = (5, 6, 7, 0)
+        FIRST_BANKS = (5, 6, 7, 0, 1, 2)
+        GRAM_BANKS = (5, 6, 7)
 
         w_planes = const.tile([P, TAPS, TAPS, O], U8, align_bytes=64)
         nc.vector.memset(w_planes[:].bitcast(I32), 0)
@@ -107,6 +108,7 @@ def tile_pvconv2d_t_e_kernel(tc, x, Wk_words, Wk_scales, bias, out):
 
         load_x(0, 1)
         load_x(1, 2)
+        load_x(3, 3)
         for j in (1, 0, 2):
             for quad in range(4):
                 nc.sync.dma_start(
@@ -118,7 +120,7 @@ def tile_pvconv2d_t_e_kernel(tc, x, Wk_words, Wk_scales, bias, out):
                 out=w_words[:, j, :, :].bitcast(I32),
                 in_=Wk_words[j :: TAPS].rearrange("i p n t -> p i (n t)").bitcast(I32),
             )
-        load_x(3, CHUNKS - 3)
+        load_x(6, 2)
         nc.sync.dma_start(out=bias_rows[:], in_=bias.partition_broadcast(P))
 
         def inverse_root(square_sum, width, name):
@@ -134,9 +136,10 @@ def tile_pvconv2d_t_e_kernel(tc, x, Wk_words, Wk_scales, bias, out):
 
         grams = {}
 
-        def gram(k):
-            grams[k] = bank_tile(AUX_BANKS, [P, B, PIX], "gram%d" % k)
-            for b in range(B):
+        def gram(k, images=range(B)):
+            if k not in grams:
+                grams[k] = bank_tile(GRAM_BANKS, [P, B, PIX], "gram%d" % k)
+            for b in images:
                 for j in range(PACK):
                     nc.tensor.matmul(
                         out=grams[k][:, b, :],
@@ -163,33 +166,12 @@ def tile_pvconv2d_t_e_kernel(tc, x, Wk_words, Wk_scales, bias, out):
                     accum_out=norm_sq[:, k, b : b + 1],
                 )
 
-        diagonals = {}
-        gram_copies = {}
-
-        def mask(k):
-            diagonals[k] = work.tile([P, B, PIX], F32, name="diagonal%d" % k, tag="diagonal")
-            nc.vector.tensor_tensor(
-                out=diagonals[k][:], in0=grams[k][:], in1=ident[:].unsqueeze(1).to_broadcast([P, B, PIX]), op=ALU.mult
-            )
-
-        def gram_out(k):
-            gram_copies[k] = work.tile([P, B, PIX], F32, name="gram_copy%d" % k, tag="gram_copy")
-            nc.scalar.copy(out=gram_copies[k][:], in_=grams[k][:])
-
-        def mask_pool(k):
-            diagonals[k] = work.tile([P, B, PIX], F32, name="diagonal%d" % k, tag="diagonal")
-            nc.gpsimd.tensor_tensor(
-                out=diagonals[k][:], in0=gram_copies[k][:], in1=ident[:].unsqueeze(1).to_broadcast([P, B, PIX]), op=ALU.mult
-            )
-
-        def reduce_vector(k):
-            nc.vector.tensor_reduce(out=norm_sq[:, k, :], in_=diagonals[k][:], axis=AXIS.X, op=ALU.add)
-
-        def reduce_scalar(k):
-            dropped = work.tile([P, B, PIX], F32, name="dropped")
+        def norm(k):
             for b in range(B):
-                nc.scalar.activation(
-                    out=dropped[:, b, :], in_=diagonals[k][:, b, :], func=ACT.Copy, accum_out=norm_sq[:, k, b : b + 1]
+                masked = work.tile([P, PIX], F32, name="masked")
+                nc.vector.scalar_tensor_tensor(
+                    out=masked[:], in0=grams[k][:, b, :], scalar=1.0, in1=ident[:], op0=ALU.mult, op1=ALU.mult,
+                    accum_out=norm_sq[:, k, b : b + 1],
                 )
 
         def log_chain(k0, k1):
@@ -414,50 +396,40 @@ def tile_pvconv2d_t_e_kernel(tc, x, Wk_words, Wk_scales, bias, out):
 
         norm_by_image(0)
         log_chain(0, 1)
-        gram(1)
-        mask(1)
-        reduce_scalar(1)
-        gram(2)
+        norm_by_image(1)
+        norm_by_image(2)
+        log_chain(1, 3)
         spread(0)
         multiply(0)
-        log_chain(1, 2)
+        for k in (3, 4, 5):
+            gram(k)
+        spread(1)
+        spread(2)
         quant(0)
         shift(0)
-        mask(2)
-        reduce_scalar(2)
-        spread(1)
         multiply(1)
-        log_chain(2, 3)
+        norm(3)
+        log_chain(3, 4)
+        quant(1)
+        shift(1)
+        norm(4)
+        norm(5)
+        multiply(2)
+        log_chain(4, 6)
         flips = []
         for k in range(CHUNKS):
             free = k + 2 >= CHUNKS
             conv(k, 0, 2)
             if k == 0:
-                gram(3)
-                quant(1)
-                shift(1)
-                mask(3)
-                reduce_scalar(3)
-                gram(4)
-                bias_add(k, 0, 2)
-                mask(4)
-                reduce_scalar(4)
-                log_chain(3, 5)
-                relu_sq(k, 0, 2, True)
-                gram(5)
-                spread(2)
-                multiply(2)
-                mask(5)
-                reduce_scalar(5)
                 gram(6)
-                mask(6)
-                reduce_scalar(6)
                 gram(7)
+                bias_add(k, 0, 2)
                 quant(2)
                 shift(2)
-                mask(7)
-                reduce_scalar(7)
-                log_chain(5, 8)
+                relu_sq(k, 0, 2, True)
+                norm(6)
+                norm(7)
+                log_chain(6, 8)
                 tanh_ones = const.tile([P, 1], F32)
                 nc.scalar.activation(out=tanh_ones[:], in_=ones[:], func=ACT.Tanh)
             else:

@@ -27,9 +27,8 @@ CURV = 0.01
 MIN_SQ = 1e-16
 MAX_Z = 1.0 - 1e-6
 
-HEAD_NORMS = 4
 DVE_SHIFTS = 1
-FLIP_LAG = 2
+SCALAR_SQ = 4
 
 FLOPS = 2 * B * H * W * C * O * TAPS * TAPS
 
@@ -57,7 +56,7 @@ def tile_pvconv2d_t_e_kernel(tc, x, Wk_words, Wk_scales, bias, out):
         AUX_BANKS = (5, 6, 7)
         END_BANKS = (3, 4, 5, 6, 7)
         FIRST_BANKS = (5, 6, 7, 0, 1, 2)
-        GRAM_BANKS = (5, 6, 7)
+        GRAM_BANKS = (5, 6, 7, 2, 5)
 
         w_planes = const.tile([P, TAPS, TAPS, O], U8, align_bytes=64)
         nc.vector.memset(w_planes[:].bitcast(I32), 0)
@@ -138,7 +137,7 @@ def tile_pvconv2d_t_e_kernel(tc, x, Wk_words, Wk_scales, bias, out):
 
         def gram(k, images=range(B)):
             if k not in grams:
-                grams[k] = bank_tile(GRAM_BANKS, [P, B, PIX], "gram%d" % k)
+                grams[k] = bank_tile(GRAM_BANKS[k - 3 : k - 2], [P, B, PIX], "gram%d" % k)
             for b in images:
                 for j in range(PACK):
                     nc.tensor.matmul(
@@ -287,67 +286,62 @@ def tile_pvconv2d_t_e_kernel(tc, x, Wk_words, Wk_scales, bias, out):
                 op=ALU.add,
             )
 
-        def relu_sq(k, r0, r1, on_vector=False):
-            squares = work.tile([P, 2, O], F32, name="squares")
-            if on_vector:
-                for r in range(r0, r1):
-                    nc.vector.scalar_tensor_tensor(
-                        out=squares[:, r - r0, :],
-                        in0=biased[k][:, r, :],
-                        scalar=0.0,
-                        in1=biased[k][:, r, :],
-                        op0=ALU.max,
-                        op1=ALU.mult,
-                        accum_out=out_norm_sq[k][:, r : r + 1],
-                    )
-                return
-            relu = work.tile([P, 2, O], F32, name="relu")
-            nc.scalar.activation(out=relu[:, 0 : r1 - r0, :], in_=biased[k][:, r0:r1, :], func=ACT.Relu)
+        def relu_sq(k, r):
+            squares = work.tile([P, O], F32, name="squares")
+            nc.vector.scalar_tensor_tensor(
+                out=squares[:], in0=biased[k][:, r, :], scalar=0.0, in1=biased[k][:, r, :], op0=ALU.max, op1=ALU.mult,
+                accum_out=out_norm_sq[k][:, r : r + 1],
+            )
+
+        def relu_sq_scalar(k, r0, r1):
+            relu = work.tile([P, r1 - r0, O], F32, name="relu")
+            nc.scalar.activation(out=relu[:], in_=biased[k][:, r0:r1, :], func=ACT.Relu)
             for r in range(r0, r1):
+                dropped = work.tile([P, O], F32, name="dropped")
                 nc.scalar.activation(
-                    out=squares[:, r - r0, :],
-                    in_=relu[:, r - r0, :],
-                    func=ACT.Square,
-                    accum_out=out_norm_sq[k][:, r : r + 1],
+                    out=dropped[:], in_=relu[:, r - r0, :], func=ACT.Square, accum_out=out_norm_sq[k][:, r : r + 1]
                 )
 
-        exp_factor = {}
         exp_parts = {}
+        exp_factor = {}
 
-        def exp_chain_a(k, r0, r1, short=False):
-            width = r1 - r0
-            y_sq = small.tile([P, width], F32, name="y_sq")
-            nc.gpsimd.tensor_scalar(
+        def exp_floor(k, r0, r1):
+            y_sq = held.tile([P, r1 - r0], F32, name="y_sq%d_%d" % (k, r0), tag="y_sq")
+            nc.vector.tensor_scalar(
                 out=y_sq[:], in0=out_norm_sq[k][:, r0:r1], scalar1=CURV, scalar2=MIN_SQ, op0=ALU.mult, op1=ALU.max
             )
+            exp_parts[(k, r0)] = y_sq
+
+        def exp_root(k, r0, r1, short=False):
+            width = r1 - r0
+            y_sq = exp_parts[(k, r0)]
             y_inv = held.tile([P, width], F32, name="y_inv%d_%d" % (k, r0), tag="y_inv")
             nc.gpsimd.tensor_tensor(out=y_inv[:], in0=y_sq[:], in1=minus_half[:, 0:width], op=ALU.pow)
             if not short:
-                y = small.tile([P, width], F32, name="y")
+                y = held.tile([P, width], F32, name="y%d_%d" % (k, r0), tag="y")
                 nc.gpsimd.tensor_tensor(out=y[:], in0=y_sq[:], in1=y_inv[:], op=ALU.mult)
                 y_sq = y
             exp_parts[(k, r0)] = (y_sq, y_inv)
 
-        def exp_chain_b(k, r0, r1, short=False):
-            y_sq, y_inv = exp_parts[(k, r0)]
+        def exp_tanh(k, r0, r1, short=False):
+            y, y_inv = exp_parts[(k, r0)]
             tanh_y = held.tile([P, r1 - r0], F32, name="tanh_y%d_%d" % (k, r0), tag="tanh_y")
             if short:
                 for r in range(r1 - r0):
                     nc.scalar.activation(
-                        out=tanh_y[:, r : r + 1], in_=y_sq[:, r : r + 1], func=ACT.Tanh, scale=y_inv[:, r : r + 1]
+                        out=tanh_y[:, r : r + 1], in_=y[:, r : r + 1], func=ACT.Tanh, scale=y_inv[:, r : r + 1]
                     )
             else:
-                nc.scalar.activation(out=tanh_y[:], in_=y_sq[:], func=ACT.Tanh)
-            exp_parts[(k, r0)] = (tanh_y, y_inv)
-            if not short:
+                nc.scalar.activation(out=tanh_y[:], in_=y[:], func=ACT.Tanh)
                 exp_factor[(k, r0)] = held.tile([P, r1 - r0], F32, name="exp_factor%d_%d" % (k, r0), tag="exp_factor")
                 nc.gpsimd.tensor_tensor(out=exp_factor[(k, r0)][:], in0=tanh_y[:], in1=y_inv[:], op=ALU.mult)
+            exp_parts[(k, r0)] = (tanh_y, y_inv)
 
         scaled = {}
 
         def rescale(k, r0, r1, on_vector=False):
             if r0 == 0:
-                scaled[k] = work.tile([P, ROWS, O], F32, name="scaled%d" % k, tag="scaled")
+                scaled[k] = work.tile([P, ROWS, O], F32, name="scaled%d" % k, tag="scaled", bufs=3)
             for r in range(r0, r1):
                 if on_vector:
                     tanh_y, y_inv = exp_parts[(k, r0)]
@@ -418,44 +412,65 @@ def tile_pvconv2d_t_e_kernel(tc, x, Wk_words, Wk_scales, bias, out):
         log_chain(4, 6)
         flips = []
         for k in range(CHUNKS):
-            free = k + 2 >= CHUNKS
             conv(k, 0, 2)
             if k == 0:
                 gram(6)
                 gram(7)
-                bias_add(k, 0, 2)
+                norm(6)
+                bias_add(0, 0, 2)
+                relu_sq_scalar(0, 0, 2)
                 quant(2)
                 shift(2)
-                relu_sq(k, 0, 2, True)
-                norm(6)
                 norm(7)
                 log_chain(6, 8)
                 tanh_ones = const.tile([P, 1], F32)
                 nc.scalar.activation(out=tanh_ones[:], in_=ones[:], func=ACT.Tanh)
             else:
                 bias_add(k - 1, 2, 4)
+                if k >= 2 and k + 2 < CHUNKS:
+                    exp_floor(k - 2, 0, ROWS)
                 if k + 2 < CHUNKS:
                     multiply(k + 2)
                 for f in flips:
                     evac(f, 0, ROWS)
                 flips.clear()
-                relu_sq(k - 1, 2, 4, True)
-                exp_chain_a(k - 1, 0, ROWS, free)
+                if k >= 2 and k + 2 < CHUNKS:
+                    exp_root(k - 2, 0, ROWS)
+                    exp_tanh(k - 2, 0, ROWS)
+                    rescale(k - 2, 0, ROWS)
+                relu_sq(k - 1, 2)
                 if k + 2 < CHUNKS:
                     quant(k + 2)
                     shift(k + 2)
+                relu_sq(k - 1, 3)
+                late = k + 3 >= CHUNKS
+                free = k + 2 >= CHUNKS
+                if late:
+                    exp_floor(k - 1, 0, ROWS)
+                    exp_root(k - 1, 0, ROWS, free)
                 bias_add(k, 0, 2)
-                relu_sq(k, 0, 2, True)
-                exp_chain_b(k - 1, 0, ROWS, free)
-                rescale(k - 1, 0, ROWS, free)
+                if late:
+                    exp_tanh(k - 1, 0, ROWS, free)
+                    if k == last:
+                        rescale(k - 1, 0, ROWS, free)
+                if k <= SCALAR_SQ:
+                    relu_sq_scalar(k, 0, 2)
+                else:
+                    relu_sq(k, 0)
+                    relu_sq(k, 1)
+                if k == last:
+                    exp_floor(last, 0, 2)
+                elif late:
+                    rescale(k - 1, 0, ROWS, free)
             if k == last:
-                exp_chain_a(last, 0, 2, True)
-                exp_chain_b(last, 0, 2, True)
+                exp_root(last, 0, 2, True)
+                exp_tanh(last, 0, 2, True)
             conv(k, 2, 4)
             if k + 3 < CHUNKS:
                 spread(k + 3)
-                ready = [k - 2] if k >= 2 else []
-            elif k + 3 == CHUNKS:
+            if k < 2:
+                ready = []
+            elif k + 2 < CHUNKS:
                 ready = [k - 2]
             elif k + 2 == CHUNKS:
                 ready = [k - 2, k - 1]
@@ -465,13 +480,16 @@ def tile_pvconv2d_t_e_kernel(tc, x, Wk_words, Wk_scales, bias, out):
                 flip(f, 0, ROWS)
                 flips.append(f)
         bias_add(last, 2, 4)
-        relu_sq(last, 2, 4, True)
-        exp_chain_a(last, 2, 4, True)
+        relu_sq(last, 2)
+        relu_sq(last, 3)
+        exp_floor(last, 2, 4)
         rescale(last, 0, 2, True)
-        evac(last - 1, 0, ROWS)
-        exp_chain_b(last, 2, 4, True)
+        evac(last - 1, 0, ROWS, halves=(0,))
+        exp_root(last, 2, 4, True)
         flip(last, 0, 2)
+        evac(last - 1, 0, ROWS, True, halves=(1,))
+        exp_tanh(last, 2, 4, True)
         rescale(last, 2, 4, True)
-        evac(last, 0, 2, True)
         flip(last, 2, 4)
+        evac(last, 0, 2, True)
         evac(last, 2, 4, True)

@@ -58,9 +58,9 @@ def tile_pvconv2d_t_e_kernel(tc, x, Wk_words, Wk_scales, bias, out):
         FIRST_BANKS = (5, 6, 7, 0, 1, 2)
         GRAM_BANKS = (5, 6, 7, 2, 5)
 
-        w_planes = const.tile([P, TAPS, TAPS, O], U8, align_bytes=64)
+        w_planes = const.tile([P, TAPS, TAPS, O], U8, align_bytes=256)
         nc.vector.memset(w_planes[:].bitcast(I32), 0)
-        w_words = const.tile([P, TAPS, TAPS, O * PACK], U8, align_bytes=64)
+        w_words = const.tile([P, TAPS, TAPS, O * PACK], U8, align_bytes=256)
         bias_rows = const.tile([P, O], BF16)
         ident = const.tile([P, P], F32)
         make_identity(nc, ident[:])
@@ -76,8 +76,8 @@ def tile_pvconv2d_t_e_kernel(tc, x, Wk_words, Wk_scales, bias, out):
         words = []
         planes = []
         for v in range(TAPS):
-            words.append(const.tile([P, H * ROW_COLS], U32, name="words%d" % v, align_bytes=64))
-            planes.append(const.tile([P, H * ROW_COLS], U8, name="planes%d" % v, align_bytes=64))
+            words.append(const.tile([P, H * ROW_COLS], U32, name="words%d" % v, align_bytes=256))
+            planes.append(const.tile([P, H * ROW_COLS], U8, name="planes%d" % v, align_bytes=256))
 
         def chunk_cols(k):
             return slice(k * CHUNK_COLS, (k + 1) * CHUNK_COLS)

@@ -28,7 +28,7 @@ MIN_SQ = 1e-16
 MAX_Z = 1.0 - 1e-6
 
 DVE_SHIFTS = 1
-SCALAR_SQ = 4
+SCALAR_SQ = 2
 
 FLOPS = 2 * B * H * W * C * O * TAPS * TAPS
 

@@ -108,17 +108,30 @@ def tile_pvconv2d_t_e_kernel(tc, x, Wk_words, Wk_scales, bias, out):
         load_x(0, 1)
         load_x(1, 2)
         load_x(3, 3)
-        for j in (1, 0, 2):
-            for quad in range(4):
-                nc.sync.dma_start(
-                    out=w_planes[32 * quad : 32 * quad + 4, j, :, :].bitcast(I32),
-                    in_=Wk_scales[j :: TAPS, 4 * quad : 4 * quad + 4, :].rearrange("i r n -> r i n").bitcast(I32),
-                )
-        for j in (1, 0, 2):
+        for quad in range(4):
             nc.sync.dma_start(
-                out=w_words[:, j, :, :].bitcast(I32),
-                in_=Wk_words[j :: TAPS].rearrange("i p n t -> p i (n t)").bitcast(I32),
+                out=w_planes[32 * quad : 32 * quad + 4, 1, :, :].bitcast(I32),
+                in_=Wk_scales[1 :: TAPS, 4 * quad : 4 * quad + 4, :].rearrange("i r n -> r i n").bitcast(I32),
             )
+        nc.sync.dma_start(
+            out=w_words[:, 1, :, :].bitcast(I32), in_=Wk_words[1 :: TAPS].rearrange("i p n t -> p i (n t)").bitcast(I32)
+        )
+        for quad in range(4):
+            nc.sync.dma_start(
+                out=w_planes[32 * quad : 32 * quad + 4, 0, :, :].bitcast(I32),
+                in_=Wk_scales[0 :: TAPS, 4 * quad : 4 * quad + 4, :].rearrange("i r n -> r i n").bitcast(I32),
+            )
+        nc.sync.dma_start(
+            out=w_words[:, 0, :, :].bitcast(I32), in_=Wk_words[0 :: TAPS].rearrange("i p n t -> p i (n t)").bitcast(I32)
+        )
+        for quad in range(4):
+            nc.sync.dma_start(
+                out=w_planes[32 * quad : 32 * quad + 4, 2, :, :].bitcast(I32),
+                in_=Wk_scales[2 :: TAPS, 4 * quad : 4 * quad + 4, :].rearrange("i r n -> r i n").bitcast(I32),
+            )
+        nc.sync.dma_start(
+            out=w_words[:, 2, :, :].bitcast(I32), in_=Wk_words[2 :: TAPS].rearrange("i p n t -> p i (n t)").bitcast(I32)
+        )
         load_x(6, 2)
         nc.sync.dma_start(out=bias_rows[:], in_=bias.partition_broadcast(P))
 
@@ -257,6 +270,8 @@ def tile_pvconv2d_t_e_kernel(tc, x, Wk_words, Wk_scales, bias, out):
                 if h + 2 < H:
                     passes.append((h + 2, j, 2, 3))
             passes.append((h + 1, 2, 1, 3))
+            if k == 0 and r0 == 0:
+                passes = [p for j in (1, 0, 2) for p in passes if p[1] == j]
             for n, (s, j, i0, i1) in enumerate(passes):
                 cols = slice(s * ROW_COLS, (s + 1) * ROW_COLS)
                 if i1 - i0 == 2:

from contextlib import ExitStack

from concourse import mybir
from concourse.masks import make_identity

F32 = mybir.dt.float32
BF16 = mybir.dt.bfloat16
I32 = mybir.dt.int32
U32 = mybir.dt.uint32
U8 = mybir.dt.uint8
FP8X4 = mybir.dt.float8_e4m3fn_x4
ALU = mybir.AluOpType
ACT = mybir.ActivationFunctionType
AXIS = mybir.AxisListType

B, C, O, H, W = 4, 512, 256, 32, 32
TAPS = 3
P = 128
PACK = 4
ROWS = 4
CHUNKS = H // ROWS
PIX = ROWS * W
ROW_COLS = W * B
CHUNK_COLS = ROWS * ROW_COLS
O_HALVES = O // P
CURV = 0.01
MIN_SQ = 1e-16
MAX_Z = 1.0 - 1e-6

DVE_SHIFTS = 1
SCALAR_SQ = 2

FLOPS = 2 * B * H * W * C * O * TAPS * TAPS


def tile_pvconv2d_t_e_kernel(tc, x, Wk_words, Wk_scales, bias, out):
    nc = tc.nc
    with ExitStack() as stack:
        const = stack.enter_context(tc.tile_pool(name="const", bufs=1))
        small = stack.enter_context(tc.tile_pool(name="small", bufs=3))
        work = stack.enter_context(tc.tile_pool(name="work", bufs=2))
        held = stack.enter_context(tc.tile_pool(name="held", bufs=4))
        stores = stack.enter_context(tc.tile_pool(name="stores", bufs=8))
        psum = stack.enter_context(tc.psum_pool(name="psum", bufs=1))
        stack.enter_context(tc.manual_schedule())

        turns = {}

        def bank_tile(banks, shape, name):
            turn = turns.get(banks, 0)
            turns[banks] = turn + 1
            return psum.tile(shape, F32, name=name, tag="bank%d" % banks[turn % len(banks)])

        ACC_BANKS = (0, 1, 2)
        SPREAD_BANKS = (3, 4)
        AUX_BANKS = (5, 6, 7)
        END_BANKS = (3, 4, 5, 6, 7)
        FIRST_BANKS = (5, 6, 7, 0, 1, 2)
        GRAM_BANKS = (5, 6, 7, 2, 5)

        w_planes = const.tile([P, TAPS, TAPS, O], U8, align_bytes=256)
        nc.vector.memset(w_planes[:].bitcast(I32), 0)
        w_words = const.tile([P, TAPS, TAPS, O * PACK], U8, align_bytes=256)
        bias_rows = const.tile([P, O], BF16)
        ident = const.tile([P, P], F32)
        make_identity(nc, ident[:])
        minus_half = const.tile([P, 4 * B], F32)
        nc.vector.memset(minus_half[:], -0.5)
        ones = const.tile([P, 1], F32)
        nc.vector.memset(ones[:], 1.0)
        ln_ones = const.tile([P, 1], F32)
        nc.scalar.activation(out=ln_ones[:], in_=ones[:], func=ACT.Ln)
        norm_sq = const.tile([P, CHUNKS, B], F32)
        log_factor = const.tile([P, CHUNKS, B], F32)

        words = []
        planes = []
        for v in range(TAPS):
            words.append(const.tile([P, H * ROW_COLS], U32, name="words%d" % v, align_bytes=256))
            planes.append(const.tile([P, H * ROW_COLS], U8, name="planes%d" % v, align_bytes=256))

        def chunk_cols(k):
            return slice(k * CHUNK_COLS, (k + 1) * CHUNK_COLS)

        def word_rows(v, k):
            return words[v][:, chunk_cols(k)].bitcast(I32).rearrange("p (r n) -> p r n", r=ROWS)

        def plane_rows(v, k):
            return planes[v][:, chunk_cols(k)].bitcast(I32).rearrange("p (r n) -> p r n", r=ROWS)

        nc.vector.memset(words[0][:].bitcast(I32).rearrange("p (h n) -> p h n", h=H)[:, :, 0:B], 0)
        nc.vector.memset(planes[0][:].bitcast(I32).rearrange("p (h n) -> p h n", h=H)[:, :, 0:1], 0)
        nc.vector.memset(words[2][:].bitcast(I32).rearrange("p (h n) -> p h n", h=H)[:, :, ROW_COLS - B : ROW_COLS], 0)
        nc.vector.memset(planes[2][:].bitcast(I32).rearrange("p (h n) -> p h n", h=H)[:, :, W - 1 : W], 0)

        x_chunks = {}

        def load_x(k, count):
            x_tile = const.tile([P, B, PACK, count * PIX], BF16, name="x_tile%d" % k)
            for b in range(B):
                nc.sync.dma_start(
                    out=x_tile[:, b, :, :],
                    in_=x[b].rearrange("(p j) h w -> p j (h w)", j=PACK)[:, :, k * PIX : (k + count) * PIX],
                )
            for n in range(count):
                x_chunks[k + n] = x_tile[:, :, :, n * PIX : (n + 1) * PIX]

        load_x(0, 1)
        load_x(1, 2)
        load_x(3, 3)
        for quad in range(4):
            nc.sync.dma_start(
                out=w_planes[32 * quad : 32 * quad + 4, 1, :, :].bitcast(I32),
                in_=Wk_scales[1 :: TAPS, 4 * quad : 4 * quad + 4, :].rearrange("i r n -> r i n").bitcast(I32),
            )
        nc.sync.dma_start(
            out=w_words[:, 1, :, :].bitcast(I32), in_=Wk_words[1 :: TAPS].rearrange("i p n t -> p i (n t)").bitcast(I32)
        )
        for quad in range(4):
            nc.sync.dma_start(
                out=w_planes[32 * quad : 32 * quad + 4, 0, :, :].bitcast(I32),
                in_=Wk_scales[0 :: TAPS, 4 * quad : 4 * quad + 4, :].rearrange("i r n -> r i n").bitcast(I32),
            )
        nc.sync.dma_start(
            out=w_words[:, 0, :, :].bitcast(I32), in_=Wk_words[0 :: TAPS].rearrange("i p n t -> p i (n t)").bitcast(I32)
        )
        for quad in range(4):
            nc.sync.dma_start(
                out=w_planes[32 * quad : 32 * quad + 4, 2, :, :].bitcast(I32),
                in_=Wk_scales[2 :: TAPS, 4 * quad : 4 * quad + 4, :].rearrange("i r n -> r i n").bitcast(I32),
            )
        nc.sync.dma_start(
            out=w_words[:, 2, :, :].bitcast(I32), in_=Wk_words[2 :: TAPS].rearrange("i p n t -> p i (n t)").bitcast(I32)
        )
        load_x(6, 2)
        nc.sync.dma_start(out=bias_rows[:], in_=bias.partition_broadcast(P))

        def inverse_root(square_sum, width, name):
            y_sq = small.tile([P, width], F32, name=name + "_sq")
            nc.gpsimd.tensor_scalar(
                out=y_sq[:], in0=square_sum, scalar1=CURV, scalar2=MIN_SQ, op0=ALU.mult, op1=ALU.max
            )
            y_inv = small.tile([P, width], F32, name=name + "_inv")
            nc.gpsimd.tensor_tensor(out=y_inv[:], in0=y_sq[:], in1=minus_half[:, 0:width], op=ALU.pow)
            y = small.tile([P, width], F32, name=name)
            nc.gpsimd.tensor_tensor(out=y[:], in0=y_sq[:], in1=y_inv[:], op=ALU.mult)
            return y, y_inv

        grams = {}

        def gram(k, images=range(B)):
            if k not in grams:
                grams[k] = bank_tile(GRAM_BANKS[k - 3 : k - 2], [P, B, PIX], "gram%d" % k)
            for b in images:
                for j in range(PACK):
                    nc.tensor.matmul(
                        out=grams[k][:, b, :],
                        lhsT=x_chunks[k][:, b, j, :],
                        rhs=x_chunks[k][:, b, j, :],
                        start=(j == 0),
                        stop=(j == PACK - 1),
                    )

        def norm_by_image(k):
            for b in range(B):
                gram_b = bank_tile(FIRST_BANKS, [P, PIX], "gram%d_%d" % (k, b))
                for j in range(PACK):
                    nc.tensor.matmul(
                        out=gram_b[:],
                        lhsT=x_chunks[k][:, b, j, :],
                        rhs=x_chunks[k][:, b, j, :],
                        start=(j == 0),
                        stop=(j == PACK - 1),
                    )
                masked = work.tile([P, PIX], F32, name="masked")
                nc.vector.scalar_tensor_tensor(
                    out=masked[:], in0=gram_b[:], scalar=1.0, in1=ident[:], op0=ALU.mult, op1=ALU.mult,
                    accum_out=norm_sq[:, k, b : b + 1],
                )

        def norm(k):
            for b in range(B):
                masked = work.tile([P, PIX], F32, name="masked")
                nc.vector.scalar_tensor_tensor(
                    out=masked[:], in0=grams[k][:, b, :], scalar=1.0, in1=ident[:], op0=ALU.mult, op1=ALU.mult,
                    accum_out=norm_sq[:, k, b : b + 1],
                )

        def log_chain(k0, k1):
            width = (k1 - k0) * B
            z, z_inv = inverse_root(norm_sq[:, k0:k1, :].rearrange("p k b -> p (k b)"), width, "z")
            z_clip = small.tile([P, width], F32, name="z_clip")
            nc.gpsimd.tensor_scalar(
                out=z_clip[:], in0=z[:], scalar1=MAX_Z, scalar2=0.0, op0=ALU.min, op1=ALU.max
            )
            ln_plus = small.tile([P, width], F32, name="ln_plus")
            nc.scalar.activation(out=ln_plus[:], in_=z_clip[:], func=ACT.Ln, bias=1.0, scale=1.0)
            ln_minus = small.tile([P, width], F32, name="ln_minus")
            nc.scalar.activation(out=ln_minus[:], in_=z_clip[:], func=ACT.Ln, bias=1.0, scale=-1.0)
            half_z_inv = small.tile([P, width], F32, name="half_z_inv")
            nc.gpsimd.tensor_scalar(
                out=half_z_inv[:], in0=z_inv[:], scalar1=0.5, scalar2=0.0, op0=ALU.mult, op1=ALU.add
            )
            ln_diff = small.tile([P, width], F32, name="ln_diff")
            nc.gpsimd.tensor_tensor(out=ln_diff[:], in0=ln_plus[:], in1=ln_minus[:], op=ALU.subtract)
            nc.gpsimd.tensor_tensor(
                out=log_factor[:, k0:k1, :].rearrange("p k b -> p (k b)"), in0=ln_diff[:], in1=half_z_inv[:], op=ALU.mult
            )

        RUN = 4
        spread_factor = {}

        def spread(k):
            spread_factor[k] = bank_tile(SPREAD_BANKS, [P, PIX // RUN, B, RUN], "spread%d" % k)
            for b in range(B):
                nc.tensor.transpose(
                    out=spread_factor[k][:, :, b, :],
                    in_=log_factor[:, k, b : b + 1].to_broadcast([P, P]),
                    identity=ident[:],
                )

        grouped = {}

        def multiply(k):
            grouped[k] = work.tile([P, PIX, B, PACK], BF16, name="grouped%d" % k, tag="grouped", align_bytes=64)
            nc.vector.tensor_tensor(
                out=grouped[k][:].rearrange("p (c i) b j -> p c b j i", i=RUN),
                in0=x_chunks[k].rearrange("p b j (c i) -> p c b j i", i=RUN),
                in1=spread_factor[k][:].unsqueeze(3).to_broadcast([P, PIX // RUN, B, PACK, RUN]),
                op=ALU.mult,
            )

        def quant(k):
            nc.vector.quantize_mx(
                out=words[1][:, chunk_cols(k)].bitcast(FP8X4),
                scales=planes[1][:, chunk_cols(k)],
                in_=grouped[k][:].rearrange("p q b j -> p (q b j)"),
            )

        def shift(k):
            moves = (
                (word_rows(0, k)[:, :, B:ROW_COLS], word_rows(1, k)[:, :, 0 : ROW_COLS - B]),
                (word_rows(2, k)[:, :, 0 : ROW_COLS - B], word_rows(1, k)[:, :, B:ROW_COLS]),
                (plane_rows(0, k)[:, :, 1:W], plane_rows(1, k)[:, :, 0 : W - 1]),
                (plane_rows(2, k)[:, :, 0 : W - 1], plane_rows(1, k)[:, :, 1:W]),
            )
            for dst, src in moves:
                if k < DVE_SHIFTS:
                    nc.vector.tensor_copy(out=dst, in_=src)
                else:
                    nc.sync.dma_start(out=dst, in_=src)

        biased = {}
        out_norm_sq = {}
        accs = {}

        def conv(k, r0, r1):
            acc = bank_tile(ACC_BANKS, [P, 2, O], "acc%d_%d" % (k, r0))
            accs[(k, r0)] = acc
            h = k * ROWS + r0
            passes = []
            for j in (1, 0, 2):
                passes.append((h, j, 0, 2))
            for j in (1, 0, 2):
                if h - 1 >= 0:
                    passes.append((h - 1, j, 0, 1))
            for j in (1, 0):
                passes.append((h + 1, j, 1, 3))
            for j in (1, 0, 2):
                if h + 2 < H:
                    passes.append((h + 2, j, 2, 3))
            passes.append((h + 1, 2, 1, 3))
            if k == 0 and r0 == 0:
                passes = [p for j in (1, 0, 2) for p in passes if p[1] == j]
            for n, (s, j, i0, i1) in enumerate(passes):
                cols = slice(s * ROW_COLS, (s + 1) * ROW_COLS)
                if i1 - i0 == 2:
                    target = acc[:].rearrange("p r o -> p (r o)")
                elif s < h:
                    target = acc[:, 1, :]
                else:
                    target = acc[:, 0, :]
                nc.tensor.matmul_mx(
                    out=target,
                    lhsT=words[j][:, cols].bitcast(FP8X4),
                    lhsT_scale=planes[j][:, cols],
                    rhs=w_words[:, j, i0:i1, :].rearrange("p i n -> p (i n)").bitcast(FP8X4),
                    rhs_scale=w_planes[:, j, i0:i1, :].rearrange("p i n -> p (i n)"),
                    start=(n == 0),
                    stop=(n == len(passes) - 1),
                )

        def bias_add(k, r0, r1):
            if r0 == 0:
                biased[k] = held.tile([P, ROWS, O], F32, name="biased%d" % k, tag="biased")
                out_norm_sq[k] = held.tile([P, ROWS], F32, name="out_norm_sq%d" % k, tag="out_norm_sq")
            nc.vector.tensor_tensor(
                out=biased[k][:, r0:r1, :],
                in0=accs[(k, r0)][:],
                in1=bias_rows[:].unsqueeze(1).to_broadcast([P, r1 - r0, O]),
                op=ALU.add,
            )

        def relu_sq(k, r):
            squares = work.tile([P, O], F32, name="squares")
            nc.vector.scalar_tensor_tensor(
                out=squares[:], in0=biased[k][:, r, :], scalar=0.0, in1=biased[k][:, r, :], op0=ALU.max, op1=ALU.mult,
                accum_out=out_norm_sq[k][:, r : r + 1],
            )

        def relu_sq_scalar(k, r0, r1):
            relu = work.tile([P, r1 - r0, O], F32, name="relu")
            nc.scalar.activation(out=relu[:], in_=biased[k][:, r0:r1, :], func=ACT.Relu)
            for r in range(r0, r1):
                dropped = work.tile([P, O], F32, name="dropped")
                nc.scalar.activation(
                    out=dropped[:], in_=relu[:, r - r0, :], func=ACT.Square, accum_out=out_norm_sq[k][:, r : r + 1]
                )

        exp_parts = {}
        exp_factor = {}

        def exp_floor(k, r0, r1):
            y_sq = held.tile([P, r1 - r0], F32, name="y_sq%d_%d" % (k, r0), tag="y_sq")
            nc.vector.tensor_scalar(
                out=y_sq[:], in0=out_norm_sq[k][:, r0:r1], scalar1=CURV, scalar2=MIN_SQ, op0=ALU.mult, op1=ALU.max
            )
            exp_parts[(k, r0)] = y_sq

        def exp_root(k, r0, r1, short=False):
            width = r1 - r0
            y_sq = exp_parts[(k, r0)]
            y_inv = held.tile([P, width], F32, name="y_inv%d_%d" % (k, r0), tag="y_inv")
            nc.gpsimd.tensor_tensor(out=y_inv[:], in0=y_sq[:], in1=minus_half[:, 0:width], op=ALU.pow)
            if not short:
                y = held.tile([P, width], F32, name="y%d_%d" % (k, r0), tag="y")
                nc.gpsimd.tensor_tensor(out=y[:], in0=y_sq[:], in1=y_inv[:], op=ALU.mult)
                y_sq = y
            exp_parts[(k, r0)] = (y_sq, y_inv)

        def exp_tanh(k, r0, r1, short=False):
            y, y_inv = exp_parts[(k, r0)]
            tanh_y = held.tile([P, r1 - r0], F32, name="tanh_y%d_%d" % (k, r0), tag="tanh_y")
            if short:
                for r in range(r1 - r0):
                    nc.scalar.activation(
                        out=tanh_y[:, r : r + 1], in_=y[:, r : r + 1], func=ACT.Tanh, scale=y_inv[:, r : r + 1]
                    )
            else:
                nc.scalar.activation(out=tanh_y[:], in_=y[:], func=ACT.Tanh)
                exp_factor[(k, r0)] = held.tile([P, r1 - r0], F32, name="exp_factor%d_%d" % (k, r0), tag="exp_factor")
                nc.gpsimd.tensor_tensor(out=exp_factor[(k, r0)][:], in0=tanh_y[:], in1=y_inv[:], op=ALU.mult)
            exp_parts[(k, r0)] = (tanh_y, y_inv)

        scaled = {}

        def rescale(k, r0, r1, on_vector=False):
            if r0 == 0:
                scaled[k] = work.tile([P, ROWS, O], F32, name="scaled%d" % k, tag="scaled", bufs=3)
            for r in range(r0, r1):
                if on_vector:
                    tanh_y, y_inv = exp_parts[(k, r0)]
                    nc.vector.tensor_scalar(
                        out=scaled[k][:, r, :], in0=biased[k][:, r, :], scalar1=tanh_y[:, r - r0 : r - r0 + 1],
                        scalar2=y_inv[:, r - r0 : r - r0 + 1], op0=ALU.mult, op1=ALU.mult,
                    )
                else:
                    nc.scalar.activation(
                        out=scaled[k][:, r, :], in_=biased[k][:, r, :], func=ACT.Copy,
                        scale=exp_factor[(k, r0)][:, r - r0 : r - r0 + 1],
                    )

        flipped = {}

        def flip(k, r0, r1):
            for half_o in range(O_HALVES):
                o_cols = slice(half_o * P, (half_o + 1) * P)
                flipped[(k, r0, half_o)] = bank_tile(
                    AUX_BANKS if k + 4 < CHUNKS else END_BANKS, [P, r1 - r0, ROW_COLS], "flipped%d_%d_%d" % (k, r0, half_o)
                )
                for r in range(r0, r1):
                    nc.tensor.transpose(
                        out=flipped[(k, r0, half_o)][:, r - r0, :], in_=scaled[k][:, r + 1 - 2 * (r % 2), o_cols], identity=ident[:]
                    )

        def evac(k, r0, r1, share=False, halves=(0, 1)):
            for half_o in halves:
                o_cols = slice(half_o * P, (half_o + 1) * P)
                result = stores.tile([P, B, r1 - r0, W], F32, name="result")
                turned = flipped[(k, r0, half_o)][:].rearrange("p r (w b) -> p b r w", b=B)
                if share and half_o == 1:
                    nc.vector.tensor_scalar(out=result[:], in0=turned, scalar1=0.0, scalar2=0.0, op0=ALU.max, op1=ALU.add)
                    nc.sync.dma_start(
                        out=out[:, o_cols, k * ROWS + r0 : k * ROWS + r1, :].rearrange("b p h w -> p b (h w)"),
                        in_=result[:].rearrange("p b r w -> p b (r w)"),
                    )
                else:
                    nc.scalar.activation(out=result[:], in_=turned, func=ACT.Relu)
                    nc.sync.dma_start(
                        out=out[:, o_cols, k * ROWS + r0 : k * ROWS + r1, :].rearrange("b p h w -> p b (h w)"),
                        in_=result[:].rearrange("p b r w -> p b (r w)"),
                    )

        last = CHUNKS - 1

        norm_by_image(0)
        log_chain(0, 1)
        norm_by_image(1)
        norm_by_image(2)
        log_chain(1, 3)
        spread(0)
        multiply(0)
        for k in (3, 4, 5):
            gram(k)
        spread(1)
        spread(2)
        quant(0)
        shift(0)
        multiply(1)
        norm(3)
        log_chain(3, 4)
        quant(1)
        shift(1)
        norm(4)
        norm(5)
        multiply(2)
        log_chain(4, 6)
        flips = []
        for k in range(CHUNKS):
            conv(k, 0, 2)
            if k == 0:
                gram(6)
                gram(7)
                norm(6)
                bias_add(0, 0, 2)
                relu_sq_scalar(0, 0, 2)
                quant(2)
                shift(2)
                norm(7)
                log_chain(6, 8)
                tanh_ones = const.tile([P, 1], F32)
                nc.scalar.activation(out=tanh_ones[:], in_=ones[:], func=ACT.Tanh)
            else:
                bias_add(k - 1, 2, 4)
                if k >= 2 and k + 2 < CHUNKS:
                    exp_floor(k - 2, 0, ROWS)
                if k + 2 < CHUNKS:
                    multiply(k + 2)
                for f in flips:
                    evac(f, 0, ROWS)
                flips.clear()
                if k >= 2 and k + 2 < CHUNKS:
                    exp_root(k - 2, 0, ROWS)
                    exp_tanh(k - 2, 0, ROWS)
                    rescale(k - 2, 0, ROWS)
                relu_sq(k - 1, 2)
                if k + 2 < CHUNKS:
                    quant(k + 2)
                    shift(k + 2)
                relu_sq(k - 1, 3)
                late = k + 3 >= CHUNKS
                free = k + 2 >= CHUNKS
                if late:
                    exp_floor(k - 1, 0, ROWS)
                    exp_root(k - 1, 0, ROWS, free)
                bias_add(k, 0, 2)
                if late:
                    exp_tanh(k - 1, 0, ROWS, free)
                    if k == last:
                        rescale(k - 1, 0, ROWS, free)
                if k <= SCALAR_SQ:
                    relu_sq_scalar(k, 0, 2)
                else:
                    relu_sq(k, 0)
                    relu_sq(k, 1)
                if k == last:
                    exp_floor(last, 0, 2)
                elif late:
                    rescale(k - 1, 0, ROWS, free)
            if k == last:
                exp_root(last, 0, 2, True)
                exp_tanh(last, 0, 2, True)
            conv(k, 2, 4)
            if k + 3 < CHUNKS:
                spread(k + 3)
            if k < 2:
                ready = []
            elif k + 2 < CHUNKS:
                ready = [k - 2]
            elif k + 2 == CHUNKS:
                ready = [k - 2, k - 1]
            else:
                ready = [k - 1]
            for f in ready:
                flip(f, 0, ROWS)
                flips.append(f)
        bias_add(last, 2, 4)
        relu_sq(last, 2)
        relu_sq(last, 3)
        exp_floor(last, 2, 4)
        rescale(last, 0, 2, True)
        evac(last - 1, 0, ROWS, halves=(0,))
        exp_root(last, 2, 4, True)
        flip(last, 0, 2)
        evac(last - 1, 0, ROWS, True, halves=(1,))
        exp_tanh(last, 2, 4, True)
        rescale(last, 2, 4, True)
        flip(last, 2, 4)
        evac(last, 0, 2, True)
        evac(last, 2, 4, True)
